import numpy as np
import ml_dtypes

BF16 = ml_dtypes.bfloat16


def bf(x):
    return np.asarray(x, np.float32).astype(BF16)


def f32(x):
    return np.asarray(x, np.float32)


def f64(x):
    return np.asarray(x).astype(np.float64)


def striped(idx):
    return np.tile(idx.reshape(-1, 16).T, (8, 1))


D, C, S, N = 128, 256, 1024, 128


def setup_inputs():
    return {"base": f32(0.02 * np.random.standard_normal((C, S))), "q": bf(0.4 * np.random.standard_normal((D, C))), "ex": bf(0.25 * np.random.standard_normal((D, N))), "offs": striped(np.random.permutation(S)[:N])}


def reference(base, q, ex, offs):
    idx = offs[:16].T.reshape(-1)
    e = f64(ex)
    s = (f64(q).T @ e) / np.sqrt(np.sum(e * e, axis=0, keepdims=True))
    l1 = np.sum(np.abs(s * s * s), axis=1, keepdims=True)
    out = f64(base).copy()
    out[:, idx] = (s * s / l1) * s
    return out

@@ -1,0 +1,66 @@
+import concourse.mybir as mybir
+
+F32 = mybir.dt.float32
+BF16 = mybir.dt.bfloat16
+U16 = mybir.dt.uint16
+MULT = mybir.AluOpType.mult
+ACT = mybir.ActivationFunctionType
+
+P = 128
+D, C, S, N = 128, 256, 1024, 128
+BLOCKS = C // P
+
+FLOPS = 2 * D * C * N + 2 * D * N
+
+
+def tile_minerva_kernel(tc, base, q, ex, offs, out):
+    nc = tc.nc
+    with (
+        tc.tile_pool(name="held", bufs=1) as held,
+        tc.psum_pool(name="psum", bufs=1) as psum,
+    ):
+        ex_sb = held.tile([D, N], BF16, name="ex_sb")
+        nc.sync.dma_start(ex_sb[:], ex)
+        q_sb = held.tile([D, C], BF16, name="q_sb")
+        nc.scalar.dma_start(q_sb[:], q)
+        offsets = held.tile([P, N // 16], U16, name="offsets")
+        nc.sync.dma_start(offsets[:], offs)
+        windows = [held.tile([P, S], F32, name=f"window{b}") for b in range(BLOCKS)]
+        nc.sync.dma_start(windows[0][:], base[0:P, :])
+        nc.scalar.dma_start(windows[1][:], base[P : 2 * P, :])
+
+        ones = held.tile([D, P], BF16, name="ones")
+        nc.gpsimd.memset(ones[:], 1.0)
+        ex_sq = held.tile([D, N], BF16, name="ex_sq")
+        nc.vector.tensor_tensor(ex_sq[:], ex_sb[:], ex_sb[:], MULT)
+        norm2 = psum.tile([P, N], F32, name="norm2")
+        nc.tensor.matmul(norm2[:], ones[:], ex_sq[:], start=True, stop=True)
+
+        dots = psum.tile([P, BLOCKS, N], F32, name="dots")
+        for k in range(BLOCKS):
+            nc.tensor.matmul(dots[:, k, :], q_sb[:, k * P : (k + 1) * P], ex_sb[:], start=True, stop=True)
+
+        inv_norm = held.tile([P, N], F32, name="inv_norm")
+        nc.scalar.activation(inv_norm[:], norm2[:], ACT.Abs_reciprocal_sqrt)
+
+        s = held.tile([P, BLOCKS, N], F32, name="s")
+        nc.vector.tensor_tensor(s[:], dots[:], inv_norm[:].unsqueeze(1).to_broadcast([P, BLOCKS, N]), MULT)
+
+        s_sq = held.tile([P, BLOCKS, N], F32, name="s_sq")
+        nc.vector.tensor_tensor(s_sq[:], s[:], s[:], MULT)
+        s_abs = held.tile([P, BLOCKS, N], F32, name="s_abs")
+        nc.scalar.activation(s_abs[:], s[:], ACT.Abs)
+        cubes = held.tile([P, BLOCKS, N], F32, name="cubes")
+        nc.vector.tensor_tensor(cubes[:], s_sq[:], s_abs[:], MULT)
+        l1 = held.tile([P, BLOCKS], F32, name="l1")
+        nc.vector.reduce_sum(l1[:], cubes[:], axis=mybir.AxisListType.X)
+        inv_l1 = held.tile([P, BLOCKS], F32, name="inv_l1")
+        nc.vector.reciprocal(inv_l1[:], l1[:])
+
+        t = held.tile([P, BLOCKS, N], F32, name="t")
+        for k in range(BLOCKS):
+            nc.vector.tensor_scalar_mul(t[:, k, :], s_sq[:, k, :], inv_l1[:, k : k + 1])
+
+        for k in range(BLOCKS):
+            nc.vector.tensor_tensor(windows[k][:].indirect(offsets[:]), t[:, k, :], s[:, k, :], MULT)
+            nc.sync.dma_start(out[k * P : (k + 1) * P, :], windows[k][:])

@@ -43,24 +43,29 @@ def tile_minerva_kernel(tc, base, q, ex, offs, out):
         inv_norm = held.tile([P, N], F32, name="inv_norm")
         nc.scalar.activation(inv_norm[:], norm2[:], ACT.Abs_reciprocal_sqrt)
 
-        s = held.tile([P, BLOCKS, N], F32, name="s")
-        nc.vector.tensor_tensor(s[:], dots[:], inv_norm[:].unsqueeze(1).to_broadcast([P, BLOCKS, N]), MULT)
+        blocks = range(BLOCKS)
+        s = [held.tile([P, N], F32, name=f"s{k}") for k in blocks]
+        s_sq = [held.tile([P, N], F32, name=f"s_sq{k}") for k in blocks]
+        s_abs = [held.tile([P, N], F32, name=f"s_abs{k}") for k in blocks]
+        cubes = [held.tile([P, N], F32, name=f"cubes{k}") for k in blocks]
+        l1 = [held.tile([P, 1], F32, name=f"l1_{k}") for k in blocks]
+        inv_l1 = [held.tile([P, 1], F32, name=f"inv_l1_{k}") for k in blocks]
+        t = [held.tile([P, N], F32, name=f"t{k}") for k in blocks]
 
-        s_sq = held.tile([P, BLOCKS, N], F32, name="s_sq")
-        nc.vector.tensor_tensor(s_sq[:], s[:], s[:], MULT)
-        s_abs = held.tile([P, BLOCKS, N], F32, name="s_abs")
-        nc.scalar.activation(s_abs[:], s[:], ACT.Abs)
-        cubes = held.tile([P, BLOCKS, N], F32, name="cubes")
-        nc.vector.tensor_tensor(cubes[:], s_sq[:], s_abs[:], MULT)
-        l1 = held.tile([P, BLOCKS], F32, name="l1")
-        nc.vector.reduce_sum(l1[:], cubes[:], axis=mybir.AxisListType.X)
-        inv_l1 = held.tile([P, BLOCKS], F32, name="inv_l1")
-        nc.vector.reciprocal(inv_l1[:], l1[:])
+        for k in blocks:
+            nc.vector.tensor_tensor(s[k][:], dots[:, k, :], inv_norm[:], MULT)
+        for k in blocks:
+            nc.scalar.activation(s_abs[k][:], s[k][:], ACT.Abs)
+            nc.vector.tensor_tensor(s_sq[k][:], s[k][:], s[k][:], MULT)
+        for k in blocks:
+            nc.vector.tensor_tensor(cubes[k][:], s_sq[k][:], s_abs[k][:], MULT)
+        for k in blocks:
+            nc.vector.reduce_sum(l1[k][:], cubes[k][:], axis=mybir.AxisListType.X)
+        for k in blocks:
+            nc.vector.reciprocal(inv_l1[k][:], l1[k][:])
+        for k in blocks:
+            nc.vector.tensor_scalar_mul(t[k][:], s_sq[k][:], inv_l1[k][:])
 
-        t = held.tile([P, BLOCKS, N], F32, name="t")
-        for k in range(BLOCKS):
-            nc.vector.tensor_scalar_mul(t[:, k, :], s_sq[:, k, :], inv_l1[:, k : k + 1])
-
-        for k in range(BLOCKS):
-            nc.vector.tensor_tensor(windows[k][:].indirect(offsets[:]), t[:, k, :], s[:, k, :], MULT)
+        for k in blocks:
+            nc.vector.tensor_tensor(windows[k][:].indirect(offsets[:]), t[k][:], s[k][:], MULT)
             nc.sync.dma_start(out[k * P : (k + 1) * P, :], windows[k][:])

@@ -58,9 +58,7 @@ def tile_minerva_kernel(tc, base, q, ex, offs, out):
             nc.scalar.activation(s_abs[k][:], s[k][:], ACT.Abs)
             nc.vector.tensor_tensor(s_sq[k][:], s[k][:], s[k][:], MULT)
         for k in blocks:
-            nc.vector.tensor_tensor(cubes[k][:], s_sq[k][:], s_abs[k][:], MULT)
-        for k in blocks:
-            nc.vector.reduce_sum(l1[k][:], cubes[k][:], axis=mybir.AxisListType.X)
+            nc.vector.scalar_tensor_tensor(cubes[k][:], s_sq[k][:], 1.0, s_abs[k][:], MULT, MULT, accum_out=l1[k][:])
         for k in blocks:
             nc.vector.reciprocal(inv_l1[k][:], l1[k][:])
         for k in blocks:

@@ -15,6 +15,7 @@ FLOPS = 2 * D * C * N + 2 * D * N
 
 def tile_minerva_kernel(tc, base, q, ex, offs, out):
     nc = tc.nc
+    blocks = range(BLOCKS)
     with (
         tc.tile_pool(name="held", bufs=1) as held,
         tc.psum_pool(name="psum", bufs=1) as psum,
@@ -25,7 +26,7 @@ def tile_minerva_kernel(tc, base, q, ex, offs, out):
         nc.scalar.dma_start(q_sb[:], q)
         offsets = held.tile([P, N // 16], U16, name="offsets")
         nc.sync.dma_start(offsets[:], offs)
-        windows = [held.tile([P, S], F32, name=f"window{b}") for b in range(BLOCKS)]
+        windows = [held.tile([P, S], F32, name=f"window{k}") for k in blocks]
         nc.sync.dma_start(windows[0][:], base[0:P, :])
         nc.scalar.dma_start(windows[1][:], base[P : 2 * P, :])
 
@@ -33,36 +34,53 @@ def tile_minerva_kernel(tc, base, q, ex, offs, out):
         nc.gpsimd.memset(ones[:], 1.0)
         ex_sq = held.tile([D, N], BF16, name="ex_sq")
         nc.vector.tensor_tensor(ex_sq[:], ex_sb[:], ex_sb[:], MULT)
+
+        dot_t = [psum.tile([N, P], F32, name=f"dot_t{k}") for k in blocks]
+        nc.tensor.matmul(dot_t[0][:], ex_sb[:], q_sb[:, 0:P], start=True, stop=True)
+        norm2_col = psum.tile([N, 1], F32, name="norm2_col")
+        nc.tensor.matmul(norm2_col[:], ex_sq[:], ones[:, 0:1], start=True, stop=True)
         norm2 = psum.tile([P, N], F32, name="norm2")
         nc.tensor.matmul(norm2[:], ones[:], ex_sq[:], start=True, stop=True)
+        nc.tensor.matmul(dot_t[1][:], ex_sb[:], q_sb[:, P : 2 * P], start=True, stop=True)
+        dot = psum.tile([P, BLOCKS, N], F32, name="dot")
+        for k in blocks:
+            nc.tensor.matmul(dot[:, k, :], q_sb[:, k * P : (k + 1) * P], ex_sb[:], start=True, stop=True)
 
-        dots = psum.tile([P, BLOCKS, N], F32, name="dots")
-        for k in range(BLOCKS):
-            nc.tensor.matmul(dots[:, k, :], q_sb[:, k * P : (k + 1) * P], ex_sb[:], start=True, stop=True)
-
+        table_warm = held.tile([D, 1], F32, name="table_warm")
+        nc.scalar.activation(table_warm[:], ones[:, 0:1], ACT.Abs_reciprocal_sqrt)
+        abs_t = [held.tile([N, P], F32, name=f"abs_t{k}") for k in blocks]
+        sq_t = [held.tile([N, P], F32, name=f"sq_t{k}") for k in blocks]
+        inv_norm_col = held.tile([N, 1], F32, name="inv_norm_col")
         inv_norm = held.tile([P, N], F32, name="inv_norm")
+        nc.scalar.activation(abs_t[0][:], dot_t[0][:], ACT.Abs)
+        nc.scalar.activation(sq_t[0][:], dot_t[0][:], ACT.Square)
+        nc.scalar.activation(inv_norm_col[:], norm2_col[:], ACT.Abs_reciprocal_sqrt)
         nc.scalar.activation(inv_norm[:], norm2[:], ACT.Abs_reciprocal_sqrt)
+        nc.scalar.activation(abs_t[1][:], dot_t[1][:], ACT.Abs)
+        nc.scalar.activation(sq_t[1][:], dot_t[1][:], ACT.Square)
 
-        blocks = range(BLOCKS)
+        cube_t = [held.tile([N, P], BF16, name=f"cube_t{k}") for k in blocks]
+        weight_col = held.tile([N, 1], BF16, name="weight_col")
+        l1 = [psum.tile([P, 1], F32, name=f"l1_{k}") for k in blocks]
+        inv_l1 = [held.tile([P, 1], F32, name=f"inv_l1_{k}") for k in blocks]
         s = [held.tile([P, N], F32, name=f"s{k}") for k in blocks]
         s_sq = [held.tile([P, N], F32, name=f"s_sq{k}") for k in blocks]
-        s_abs = [held.tile([P, N], F32, name=f"s_abs{k}") for k in blocks]
-        cubes = [held.tile([P, N], F32, name=f"cubes{k}") for k in blocks]
-        l1 = [held.tile([P, 1], F32, name=f"l1_{k}") for k in blocks]
-        inv_l1 = [held.tile([P, 1], F32, name=f"inv_l1_{k}") for k in blocks]
         t = [held.tile([P, N], F32, name=f"t{k}") for k in blocks]
 
+        nc.vector.tensor_tensor(cube_t[0][:], abs_t[0][:], sq_t[0][:], MULT)
+        nc.vector.scalar_tensor_tensor(weight_col[:], inv_norm_col[:], inv_norm_col[:], inv_norm_col[:], MULT, MULT)
+        nc.tensor.matmul(l1[0][:], cube_t[0][:], weight_col[:], start=True, stop=True)
         for k in blocks:
-            nc.vector.tensor_tensor(s[k][:], dots[:, k, :], inv_norm[:], MULT)
+            nc.vector.tensor_tensor(s[k][:], dot[:, k, :], inv_norm[:], MULT)
+        nc.vector.tensor_tensor(cube_t[1][:], abs_t[1][:], sq_t[1][:], MULT)
+        nc.tensor.matmul(l1[1][:], cube_t[1][:], weight_col[:], start=True, stop=True)
         for k in blocks:
-            nc.scalar.activation(s_abs[k][:], s[k][:], ACT.Abs)
             nc.vector.tensor_tensor(s_sq[k][:], s[k][:], s[k][:], MULT)
-        for k in blocks:
-            nc.vector.scalar_tensor_tensor(cubes[k][:], s_sq[k][:], 1.0, s_abs[k][:], MULT, MULT, accum_out=l1[k][:])
-        for k in blocks:
-            nc.vector.reciprocal(inv_l1[k][:], l1[k][:])
-        for k in blocks:
-            nc.vector.tensor_scalar_mul(t[k][:], s_sq[k][:], inv_l1[k][:])
+
+        nc.vector.reciprocal(inv_l1[0][:], l1[0][:])
+        nc.vector.tensor_scalar_mul(t[0][:], s_sq[0][:], inv_l1[0][:])
+        nc.vector.reciprocal(inv_l1[1][:], l1[1][:])
+        nc.scalar.activation(t[1][:], s_sq[1][:], ACT.Copy, scale=inv_l1[1][:])
 
         for k in blocks:
             nc.vector.tensor_tensor(windows[k][:].indirect(offsets[:]), t[k][:], s[k][:], MULT)

@@ -22,13 +22,14 @@ def tile_minerva_kernel(tc, base, q, ex, offs, out):
     ):
         ex_sb = held.tile([D, N], BF16, name="ex_sb")
         nc.sync.dma_start(ex_sb[:], ex)
-        q_sb = held.tile([D, C], BF16, name="q_sb")
-        nc.scalar.dma_start(q_sb[:], q)
-        offsets = held.tile([P, N // 16], U16, name="offsets")
-        nc.sync.dma_start(offsets[:], offs)
+        q_sb = [held.tile([D, P], BF16, name=f"q_sb{k}") for k in blocks]
+        nc.scalar.dma_start(q_sb[0][:], q[:, 0:P])
+        nc.sync.dma_start(q_sb[1][:], q[:, P : 2 * P])
         windows = [held.tile([P, S], F32, name=f"window{k}") for k in blocks]
         nc.sync.dma_start(windows[0][:], base[0:P, :])
         nc.scalar.dma_start(windows[1][:], base[P : 2 * P, :])
+        offsets = held.tile([P, N // 16], U16, name="offsets")
+        nc.sync.dma_start(offsets[:], offs)
 
         ones = held.tile([D, P], BF16, name="ones")
         nc.gpsimd.memset(ones[:], 1.0)
@@ -36,15 +37,15 @@ def tile_minerva_kernel(tc, base, q, ex, offs, out):
         nc.vector.tensor_tensor(ex_sq[:], ex_sb[:], ex_sb[:], MULT)
 
         dot_t = [psum.tile([N, P], F32, name=f"dot_t{k}") for k in blocks]
-        nc.tensor.matmul(dot_t[0][:], ex_sb[:], q_sb[:, 0:P], start=True, stop=True)
+        nc.tensor.matmul(dot_t[0][:], ex_sb[:], q_sb[0][:], start=True, stop=True)
         norm2_col = psum.tile([N, 1], F32, name="norm2_col")
         nc.tensor.matmul(norm2_col[:], ex_sq[:], ones[:, 0:1], start=True, stop=True)
         norm2 = psum.tile([P, N], F32, name="norm2")
         nc.tensor.matmul(norm2[:], ones[:], ex_sq[:], start=True, stop=True)
-        nc.tensor.matmul(dot_t[1][:], ex_sb[:], q_sb[:, P : 2 * P], start=True, stop=True)
+        nc.tensor.matmul(dot_t[1][:], ex_sb[:], q_sb[1][:], start=True, stop=True)
         dot = psum.tile([P, BLOCKS, N], F32, name="dot")
         for k in blocks:
-            nc.tensor.matmul(dot[:, k, :], q_sb[:, k * P : (k + 1) * P], ex_sb[:], start=True, stop=True)
+            nc.tensor.matmul(dot[:, k, :], q_sb[k][:], ex_sb[:], start=True, stop=True)
 
         table_warm = held.tile([D, 1], F32, name="table_warm")
         nc.scalar.activation(table_warm[:], ones[:, 0:1], ACT.Abs_reciprocal_sqrt)

@@ -25,11 +25,11 @@ def tile_minerva_kernel(tc, base, q, ex, offs, out):
         q_sb = [held.tile([D, P], BF16, name=f"q_sb{k}") for k in blocks]
         nc.scalar.dma_start(q_sb[0][:], q[:, 0:P])
         nc.sync.dma_start(q_sb[1][:], q[:, P : 2 * P])
-        windows = [held.tile([P, S], F32, name=f"window{k}") for k in blocks]
-        nc.sync.dma_start(windows[0][:], base[0:P, :])
-        nc.scalar.dma_start(windows[1][:], base[P : 2 * P, :])
         offsets = held.tile([P, N // 16], U16, name="offsets")
         nc.sync.dma_start(offsets[:], offs)
+        windows = [held.tile([P, S], F32, name=f"window{k}") for k in blocks]
+        nc.scalar.dma_start(windows[0][:], base[0:P, :])
+        nc.sync.dma_start(windows[1][:], base[P : 2 * P, :])
 
         ones = held.tile([D, P], BF16, name="ones")
         nc.gpsimd.memset(ones[:], 1.0)
@@ -63,25 +63,25 @@ def tile_minerva_kernel(tc, base, q, ex, offs, out):
         cube_t = [held.tile([N, P], BF16, name=f"cube_t{k}") for k in blocks]
         weight_col = held.tile([N, 1], BF16, name="weight_col")
         l1 = [psum.tile([P, 1], F32, name=f"l1_{k}") for k in blocks]
-        inv_l1 = [held.tile([P, 1], F32, name=f"inv_l1_{k}") for k in blocks]
         s = [held.tile([P, N], F32, name=f"s{k}") for k in blocks]
-        s_sq = [held.tile([P, N], F32, name=f"s_sq{k}") for k in blocks]
         t = [held.tile([P, N], F32, name=f"t{k}") for k in blocks]
+        s_sq = held.tile([P, N], F32, name="s_sq")
+        inv_l1 = held.tile([P, 1], F32, name="inv_l1")
+        inv_sqrt_l1 = held.tile([P, 1], F32, name="inv_sqrt_l1")
 
         nc.vector.tensor_tensor(cube_t[0][:], abs_t[0][:], sq_t[0][:], MULT)
         nc.vector.scalar_tensor_tensor(weight_col[:], inv_norm_col[:], inv_norm_col[:], inv_norm_col[:], MULT, MULT)
         nc.tensor.matmul(l1[0][:], cube_t[0][:], weight_col[:], start=True, stop=True)
-        for k in blocks:
-            nc.vector.tensor_tensor(s[k][:], dot[:, k, :], inv_norm[:], MULT)
+        nc.vector.tensor_tensor(s[0][:], dot[:, 0, :], inv_norm[:], MULT)
         nc.vector.tensor_tensor(cube_t[1][:], abs_t[1][:], sq_t[1][:], MULT)
         nc.tensor.matmul(l1[1][:], cube_t[1][:], weight_col[:], start=True, stop=True)
-        for k in blocks:
-            nc.vector.tensor_tensor(s_sq[k][:], s[k][:], s[k][:], MULT)
+        nc.vector.tensor_tensor(s_sq[:], s[0][:], s[0][:], MULT)
 
-        nc.vector.reciprocal(inv_l1[0][:], l1[0][:])
-        nc.vector.tensor_scalar_mul(t[0][:], s_sq[0][:], inv_l1[0][:])
-        nc.vector.reciprocal(inv_l1[1][:], l1[1][:])
-        nc.scalar.activation(t[1][:], s_sq[1][:], ACT.Copy, scale=inv_l1[1][:])
+        nc.vector.reciprocal(inv_l1[:], l1[0][:])
+        nc.vector.tensor_tensor(s[1][:], dot[:, 1, :], inv_norm[:], MULT)
+        nc.vector.tensor_scalar_mul(t[0][:], s_sq[:], inv_l1[:])
+        nc.scalar.activation(inv_sqrt_l1[:], l1[1][:], ACT.Abs_reciprocal_sqrt)
+        nc.scalar.activation(t[1][:], s[1][:], ACT.Square, scale=inv_sqrt_l1[:])
 
         for k in blocks:
             nc.vector.tensor_tensor(windows[k][:].indirect(offsets[:]), t[k][:], s[k][:], MULT)

@@ -29,7 +29,7 @@ def tile_minerva_kernel(tc, base, q, ex, offs, out):
         nc.sync.dma_start(offsets[:], offs)
         windows = [held.tile([P, S], F32, name=f"window{k}") for k in blocks]
         nc.scalar.dma_start(windows[0][:], base[0:P, :])
-        nc.sync.dma_start(windows[1][:], base[P : 2 * P, :])
+        nc.scalar.dma_start(windows[1][:], base[P : 2 * P, :])
 
         ones = held.tile([D, P], BF16, name="ones")
         nc.gpsimd.memset(ones[:], 1.0)

@@ -16,6 +16,7 @@ FLOPS = 2 * D * C * N + 2 * D * N
 def tile_minerva_kernel(tc, base, q, ex, offs, out):
     nc = tc.nc
     blocks = range(BLOCKS)
+    halves = (slice(0, P // 2), slice(P // 2, P))
     with (
         tc.tile_pool(name="held", bufs=1) as held,
         tc.psum_pool(name="psum", bufs=1) as psum,
@@ -47,39 +48,40 @@ def tile_minerva_kernel(tc, base, q, ex, offs, out):
         for k in blocks:
             nc.tensor.matmul(dot[:, k, :], q_sb[k][:], ex_sb[:], start=True, stop=True)
 
+        inv_norm2_col = held.tile([N, 1], F32, name="inv_norm2_col")
+        nc.vector.reciprocal(inv_norm2_col[:], norm2_col[:])
+
         table_warm = held.tile([D, 1], F32, name="table_warm")
         nc.scalar.activation(table_warm[:], ones[:, 0:1], ACT.Abs_reciprocal_sqrt)
         abs_t = [held.tile([N, P], F32, name=f"abs_t{k}") for k in blocks]
         sq_t = [held.tile([N, P], F32, name=f"sq_t{k}") for k in blocks]
-        inv_norm_col = held.tile([N, 1], F32, name="inv_norm_col")
+        inv_norm_col = held.tile([N, 1], BF16, name="inv_norm_col")
         inv_norm = held.tile([P, N], F32, name="inv_norm")
-        nc.scalar.activation(abs_t[0][:], dot_t[0][:], ACT.Abs)
-        nc.scalar.activation(sq_t[0][:], dot_t[0][:], ACT.Square)
+        for h in halves:
+            nc.scalar.activation(abs_t[0][:, h], dot_t[0][:, h], ACT.Abs)
+            nc.scalar.activation(sq_t[0][:, h], dot_t[0][:, h], ACT.Square)
         nc.scalar.activation(inv_norm_col[:], norm2_col[:], ACT.Abs_reciprocal_sqrt)
         nc.scalar.activation(inv_norm[:], norm2[:], ACT.Abs_reciprocal_sqrt)
         nc.scalar.activation(abs_t[1][:], dot_t[1][:], ACT.Abs)
         nc.scalar.activation(sq_t[1][:], dot_t[1][:], ACT.Square)
 
         cube_t = [held.tile([N, P], BF16, name=f"cube_t{k}") for k in blocks]
-        weight_col = held.tile([N, 1], BF16, name="weight_col")
         l1 = [psum.tile([P, 1], F32, name=f"l1_{k}") for k in blocks]
         s = [held.tile([P, N], F32, name=f"s{k}") for k in blocks]
         t = [held.tile([P, N], F32, name=f"t{k}") for k in blocks]
-        s_sq = held.tile([P, N], F32, name="s_sq")
         inv_l1 = held.tile([P, 1], F32, name="inv_l1")
         inv_sqrt_l1 = held.tile([P, 1], F32, name="inv_sqrt_l1")
 
-        nc.vector.tensor_tensor(cube_t[0][:], abs_t[0][:], sq_t[0][:], MULT)
-        nc.vector.scalar_tensor_tensor(weight_col[:], inv_norm_col[:], inv_norm_col[:], inv_norm_col[:], MULT, MULT)
-        nc.tensor.matmul(l1[0][:], cube_t[0][:], weight_col[:], start=True, stop=True)
+        for h in halves:
+            nc.vector.scalar_tensor_tensor(cube_t[0][:, h], abs_t[0][:, h], inv_norm2_col[:], sq_t[0][:, h], MULT, MULT)
+        nc.tensor.matmul(l1[0][:], cube_t[0][:], inv_norm_col[:], start=True, stop=True)
         nc.vector.tensor_tensor(s[0][:], dot[:, 0, :], inv_norm[:], MULT)
-        nc.vector.tensor_tensor(cube_t[1][:], abs_t[1][:], sq_t[1][:], MULT)
-        nc.tensor.matmul(l1[1][:], cube_t[1][:], weight_col[:], start=True, stop=True)
-        nc.vector.tensor_tensor(s_sq[:], s[0][:], s[0][:], MULT)
+        nc.vector.scalar_tensor_tensor(cube_t[1][:], abs_t[1][:], inv_norm2_col[:], sq_t[1][:], MULT, MULT)
+        nc.tensor.matmul(l1[1][:], cube_t[1][:], inv_norm_col[:], start=True, stop=True)
 
         nc.vector.reciprocal(inv_l1[:], l1[0][:])
         nc.vector.tensor_tensor(s[1][:], dot[:, 1, :], inv_norm[:], MULT)
-        nc.vector.tensor_scalar_mul(t[0][:], s_sq[:], inv_l1[:])
+        nc.vector.scalar_tensor_tensor(t[0][:], s[0][:], inv_l1[:], s[0][:], MULT, MULT)
         nc.scalar.activation(inv_sqrt_l1[:], l1[1][:], ACT.Abs_reciprocal_sqrt)
         nc.scalar.activation(t[1][:], s[1][:], ACT.Square, scale=inv_sqrt_l1[:])
 

@@ -9,6 +9,7 @@ ACT = mybir.ActivationFunctionType
 P = 128
 D, C, S, N = 128, 256, 1024, 128
 BLOCKS = C // P
+HALF = P // 2
 
 FLOPS = 2 * D * C * N + 2 * D * N
 
@@ -16,7 +17,7 @@ FLOPS = 2 * D * C * N + 2 * D * N
 def tile_minerva_kernel(tc, base, q, ex, offs, out):
     nc = tc.nc
     blocks = range(BLOCKS)
-    halves = (slice(0, P // 2), slice(P // 2, P))
+    halves = range(2)
     with (
         tc.tile_pool(name="held", bufs=1) as held,
         tc.psum_pool(name="psum", bufs=1) as psum,
@@ -37,33 +38,35 @@ def tile_minerva_kernel(tc, base, q, ex, offs, out):
         ex_sq = held.tile([D, N], BF16, name="ex_sq")
         nc.vector.tensor_tensor(ex_sq[:], ex_sb[:], ex_sb[:], MULT)
 
-        dot_t = [psum.tile([N, P], F32, name=f"dot_t{k}") for k in blocks]
-        nc.tensor.matmul(dot_t[0][:], ex_sb[:], q_sb[0][:], start=True, stop=True)
+        dot_t0 = [psum.tile([N, HALF], F32, name=f"dot_t0_{h}") for h in halves]
+        for h in halves:
+            nc.tensor.matmul(dot_t0[h][:], ex_sb[:], q_sb[0][:, h * HALF : (h + 1) * HALF], start=True, stop=True)
         norm2_col = psum.tile([N, 1], F32, name="norm2_col")
         nc.tensor.matmul(norm2_col[:], ex_sq[:], ones[:, 0:1], start=True, stop=True)
         norm2 = psum.tile([P, N], F32, name="norm2")
         nc.tensor.matmul(norm2[:], ones[:], ex_sq[:], start=True, stop=True)
-        nc.tensor.matmul(dot_t[1][:], ex_sb[:], q_sb[1][:], start=True, stop=True)
+        dot_t1 = psum.tile([N, P], F32, name="dot_t1")
+        nc.tensor.matmul(dot_t1[:], ex_sb[:], q_sb[1][:], start=True, stop=True)
         dot = psum.tile([P, BLOCKS, N], F32, name="dot")
         for k in blocks:
             nc.tensor.matmul(dot[:, k, :], q_sb[k][:], ex_sb[:], start=True, stop=True)
 
-        inv_norm2_col = held.tile([N, 1], F32, name="inv_norm2_col")
-        nc.vector.reciprocal(inv_norm2_col[:], norm2_col[:])
-
         table_warm = held.tile([D, 1], F32, name="table_warm")
         nc.scalar.activation(table_warm[:], ones[:, 0:1], ACT.Abs_reciprocal_sqrt)
-        abs_t = [held.tile([N, P], F32, name=f"abs_t{k}") for k in blocks]
-        sq_t = [held.tile([N, P], F32, name=f"sq_t{k}") for k in blocks]
-        inv_norm_col = held.tile([N, 1], BF16, name="inv_norm_col")
+        abs_t0 = [held.tile([N, HALF], F32, name=f"abs_t0_{h}") for h in halves]
+        sq_t0 = [held.tile([N, HALF], F32, name=f"sq_t0_{h}") for h in halves]
+        abs_t1 = held.tile([N, P], F32, name="abs_t1")
+        sq_t1 = held.tile([N, P], F32, name="sq_t1")
+        inv_norm_col = held.tile([N, 1], F32, name="inv_norm_col")
+        weight_col = held.tile([N, 1], BF16, name="weight_col")
         inv_norm = held.tile([P, N], F32, name="inv_norm")
         for h in halves:
-            nc.scalar.activation(abs_t[0][:, h], dot_t[0][:, h], ACT.Abs)
-            nc.scalar.activation(sq_t[0][:, h], dot_t[0][:, h], ACT.Square)
+            nc.scalar.activation(abs_t0[h][:], dot_t0[h][:], ACT.Abs)
+            nc.scalar.activation(sq_t0[h][:], dot_t0[h][:], ACT.Square)
         nc.scalar.activation(inv_norm_col[:], norm2_col[:], ACT.Abs_reciprocal_sqrt)
         nc.scalar.activation(inv_norm[:], norm2[:], ACT.Abs_reciprocal_sqrt)
-        nc.scalar.activation(abs_t[1][:], dot_t[1][:], ACT.Abs)
-        nc.scalar.activation(sq_t[1][:], dot_t[1][:], ACT.Square)
+        nc.scalar.activation(abs_t1[:], dot_t1[:], ACT.Abs)
+        nc.scalar.activation(sq_t1[:], dot_t1[:], ACT.Square)
 
         cube_t = [held.tile([N, P], BF16, name=f"cube_t{k}") for k in blocks]
         l1 = [psum.tile([P, 1], F32, name=f"l1_{k}") for k in blocks]
@@ -73,11 +76,13 @@ def tile_minerva_kernel(tc, base, q, ex, offs, out):
         inv_sqrt_l1 = held.tile([P, 1], F32, name="inv_sqrt_l1")
 
         for h in halves:
-            nc.vector.scalar_tensor_tensor(cube_t[0][:, h], abs_t[0][:, h], inv_norm2_col[:], sq_t[0][:, h], MULT, MULT)
-        nc.tensor.matmul(l1[0][:], cube_t[0][:], inv_norm_col[:], start=True, stop=True)
+            cube_half = cube_t[0][:, h * HALF : (h + 1) * HALF]
+            nc.vector.tensor_tensor(cube_half, abs_t0[h][:], sq_t0[h][:], MULT)
+        nc.vector.scalar_tensor_tensor(weight_col[:], inv_norm_col[:], inv_norm_col[:], inv_norm_col[:], MULT, MULT)
+        nc.tensor.matmul(l1[0][:], cube_t[0][:], weight_col[:], start=True, stop=True)
         nc.vector.tensor_tensor(s[0][:], dot[:, 0, :], inv_norm[:], MULT)
-        nc.vector.scalar_tensor_tensor(cube_t[1][:], abs_t[1][:], inv_norm2_col[:], sq_t[1][:], MULT, MULT)
-        nc.tensor.matmul(l1[1][:], cube_t[1][:], inv_norm_col[:], start=True, stop=True)
+        nc.vector.tensor_tensor(cube_t[1][:], abs_t1[:], sq_t1[:], MULT)
+        nc.tensor.matmul(l1[1][:], cube_t[1][:], weight_col[:], start=True, stop=True)
 
         nc.vector.reciprocal(inv_l1[:], l1[0][:])
         nc.vector.tensor_tensor(s[1][:], dot[:, 1, :], inv_norm[:], MULT)

@@ -45,11 +45,11 @@ def tile_minerva_kernel(tc, base, q, ex, offs, out):
         nc.tensor.matmul(norm2_col[:], ex_sq[:], ones[:, 0:1], start=True, stop=True)
         norm2 = psum.tile([P, N], F32, name="norm2")
         nc.tensor.matmul(norm2[:], ones[:], ex_sq[:], start=True, stop=True)
+        dot = [psum.tile([P, N], F32, name=f"dot{k}") for k in blocks]
         dot_t1 = psum.tile([N, P], F32, name="dot_t1")
+        nc.tensor.matmul(dot[0][:], q_sb[0][:], ex_sb[:], start=True, stop=True)
         nc.tensor.matmul(dot_t1[:], ex_sb[:], q_sb[1][:], start=True, stop=True)
-        dot = psum.tile([P, BLOCKS, N], F32, name="dot")
-        for k in blocks:
-            nc.tensor.matmul(dot[:, k, :], q_sb[k][:], ex_sb[:], start=True, stop=True)
+        nc.tensor.matmul(dot[1][:], q_sb[1][:], ex_sb[:], start=True, stop=True)
 
         table_warm = held.tile([D, 1], F32, name="table_warm")
         nc.scalar.activation(table_warm[:], ones[:, 0:1], ACT.Abs_reciprocal_sqrt)
@@ -69,7 +69,7 @@ def tile_minerva_kernel(tc, base, q, ex, offs, out):
         nc.scalar.activation(sq_t1[:], dot_t1[:], ACT.Square)
 
         cube_t = [held.tile([N, P], BF16, name=f"cube_t{k}") for k in blocks]
-        l1 = [psum.tile([P, 1], F32, name=f"l1_{k}") for k in blocks]
+        l1 = [psum.tile([P, 1], F32, name="l1_0"), psum.tile([P, 1], F32, name="l1_1", tag="norm2_col")]
         s = [held.tile([P, N], F32, name=f"s{k}") for k in blocks]
         t = [held.tile([P, N], F32, name=f"t{k}") for k in blocks]
         inv_l1 = held.tile([P, 1], F32, name="inv_l1")
@@ -80,12 +80,12 @@ def tile_minerva_kernel(tc, base, q, ex, offs, out):
             nc.vector.tensor_tensor(cube_half, abs_t0[h][:], sq_t0[h][:], MULT)
         nc.vector.scalar_tensor_tensor(weight_col[:], inv_norm_col[:], inv_norm_col[:], inv_norm_col[:], MULT, MULT)
         nc.tensor.matmul(l1[0][:], cube_t[0][:], weight_col[:], start=True, stop=True)
-        nc.vector.tensor_tensor(s[0][:], dot[:, 0, :], inv_norm[:], MULT)
+        nc.vector.tensor_tensor(s[0][:], dot[0][:], inv_norm[:], MULT)
         nc.vector.tensor_tensor(cube_t[1][:], abs_t1[:], sq_t1[:], MULT)
         nc.tensor.matmul(l1[1][:], cube_t[1][:], weight_col[:], start=True, stop=True)
 
         nc.vector.reciprocal(inv_l1[:], l1[0][:])
-        nc.vector.tensor_tensor(s[1][:], dot[:, 1, :], inv_norm[:], MULT)
+        nc.vector.tensor_tensor(s[1][:], dot[1][:], inv_norm[:], MULT)
         nc.vector.scalar_tensor_tensor(t[0][:], s[0][:], inv_l1[:], s[0][:], MULT, MULT)
         nc.scalar.activation(inv_sqrt_l1[:], l1[1][:], ACT.Abs_reciprocal_sqrt)
         nc.scalar.activation(t[1][:], s[1][:], ACT.Square, scale=inv_sqrt_l1[:])

@@ -31,7 +31,7 @@ def tile_minerva_kernel(tc, base, q, ex, offs, out):
         nc.sync.dma_start(offsets[:], offs)
         windows = [held.tile([P, S], F32, name=f"window{k}") for k in blocks]
         nc.scalar.dma_start(windows[0][:], base[0:P, :])
-        nc.scalar.dma_start(windows[1][:], base[P : 2 * P, :])
+        nc.sync.dma_start(windows[1][:], base[P : 2 * P, :])
 
         ones = held.tile([D, P], BF16, name="ones")
         nc.gpsimd.memset(ones[:], 1.0)

import concourse.mybir as mybir

F32 = mybir.dt.float32
BF16 = mybir.dt.bfloat16
U16 = mybir.dt.uint16
MULT = mybir.AluOpType.mult
ACT = mybir.ActivationFunctionType

P = 128
D, C, S, N = 128, 256, 1024, 128
BLOCKS = C // P
HALF = P // 2

FLOPS = 2 * D * C * N + 2 * D * N


def tile_minerva_kernel(tc, base, q, ex, offs, out):
    nc = tc.nc
    blocks = range(BLOCKS)
    halves = range(2)
    with (
        tc.tile_pool(name="held", bufs=1) as held,
        tc.psum_pool(name="psum", bufs=1) as psum,
    ):
        ex_sb = held.tile([D, N], BF16, name="ex_sb")
        nc.sync.dma_start(ex_sb[:], ex)
        q_sb = [held.tile([D, P], BF16, name=f"q_sb{k}") for k in blocks]
        nc.scalar.dma_start(q_sb[0][:], q[:, 0:P])
        nc.sync.dma_start(q_sb[1][:], q[:, P : 2 * P])
        offsets = held.tile([P, N // 16], U16, name="offsets")
        nc.sync.dma_start(offsets[:], offs)
        windows = [held.tile([P, S], F32, name=f"window{k}") for k in blocks]
        nc.scalar.dma_start(windows[0][:], base[0:P, :])
        nc.sync.dma_start(windows[1][:], base[P : 2 * P, :])

        ones = held.tile([D, P], BF16, name="ones")
        nc.gpsimd.memset(ones[:], 1.0)
        ex_sq = held.tile([D, N], BF16, name="ex_sq")
        nc.vector.tensor_tensor(ex_sq[:], ex_sb[:], ex_sb[:], MULT)

        dot_t0 = [psum.tile([N, HALF], F32, name=f"dot_t0_{h}") for h in halves]
        for h in halves:
            nc.tensor.matmul(dot_t0[h][:], ex_sb[:], q_sb[0][:, h * HALF : (h + 1) * HALF], start=True, stop=True)
        norm2_col = psum.tile([N, 1], F32, name="norm2_col")
        nc.tensor.matmul(norm2_col[:], ex_sq[:], ones[:, 0:1], start=True, stop=True)
        norm2 = psum.tile([P, N], F32, name="norm2")
        nc.tensor.matmul(norm2[:], ones[:], ex_sq[:], start=True, stop=True)
        dot = [psum.tile([P, N], F32, name=f"dot{k}") for k in blocks]
        dot_t1 = psum.tile([N, P], F32, name="dot_t1")
        nc.tensor.matmul(dot[0][:], q_sb[0][:], ex_sb[:], start=True, stop=True)
        nc.tensor.matmul(dot_t1[:], ex_sb[:], q_sb[1][:], start=True, stop=True)
        nc.tensor.matmul(dot[1][:], q_sb[1][:], ex_sb[:], start=True, stop=True)

        table_warm = held.tile([D, 1], F32, name="table_warm")
        nc.scalar.activation(table_warm[:], ones[:, 0:1], ACT.Abs_reciprocal_sqrt)
        abs_t0 = [held.tile([N, HALF], F32, name=f"abs_t0_{h}") for h in halves]
        sq_t0 = [held.tile([N, HALF], F32, name=f"sq_t0_{h}") for h in halves]
        abs_t1 = held.tile([N, P], F32, name="abs_t1")
        sq_t1 = held.tile([N, P], F32, name="sq_t1")
        inv_norm_col = held.tile([N, 1], F32, name="inv_norm_col")
        weight_col = held.tile([N, 1], BF16, name="weight_col")
        inv_norm = held.tile([P, N], F32, name="inv_norm")
        for h in halves:
            nc.scalar.activation(abs_t0[h][:], dot_t0[h][:], ACT.Abs)
            nc.scalar.activation(sq_t0[h][:], dot_t0[h][:], ACT.Square)
        nc.scalar.activation(inv_norm_col[:], norm2_col[:], ACT.Abs_reciprocal_sqrt)
        nc.scalar.activation(inv_norm[:], norm2[:], ACT.Abs_reciprocal_sqrt)
        nc.scalar.activation(abs_t1[:], dot_t1[:], ACT.Abs)
        nc.scalar.activation(sq_t1[:], dot_t1[:], ACT.Square)

        cube_t = [held.tile([N, P], BF16, name=f"cube_t{k}") for k in blocks]
        l1 = [psum.tile([P, 1], F32, name="l1_0"), psum.tile([P, 1], F32, name="l1_1", tag="norm2_col")]
        s = [held.tile([P, N], F32, name=f"s{k}") for k in blocks]
        t = [held.tile([P, N], F32, name=f"t{k}") for k in blocks]
        inv_l1 = held.tile([P, 1], F32, name="inv_l1")
        inv_sqrt_l1 = held.tile([P, 1], F32, name="inv_sqrt_l1")

        for h in halves:
            cube_half = cube_t[0][:, h * HALF : (h + 1) * HALF]
            nc.vector.tensor_tensor(cube_half, abs_t0[h][:], sq_t0[h][:], MULT)
        nc.vector.scalar_tensor_tensor(weight_col[:], inv_norm_col[:], inv_norm_col[:], inv_norm_col[:], MULT, MULT)
        nc.tensor.matmul(l1[0][:], cube_t[0][:], weight_col[:], start=True, stop=True)
        nc.vector.tensor_tensor(s[0][:], dot[0][:], inv_norm[:], MULT)
        nc.vector.tensor_tensor(cube_t[1][:], abs_t1[:], sq_t1[:], MULT)
        nc.tensor.matmul(l1[1][:], cube_t[1][:], weight_col[:], start=True, stop=True)

        nc.vector.reciprocal(inv_l1[:], l1[0][:])
        nc.vector.tensor_tensor(s[1][:], dot[1][:], inv_norm[:], MULT)
        nc.vector.scalar_tensor_tensor(t[0][:], s[0][:], inv_l1[:], s[0][:], MULT, MULT)
        nc.scalar.activation(inv_sqrt_l1[:], l1[1][:], ACT.Abs_reciprocal_sqrt)
        nc.scalar.activation(t[1][:], s[1][:], ACT.Square, scale=inv_sqrt_l1[:])

        for k in blocks:
            nc.vector.tensor_tensor(windows[k][:].indirect(offsets[:]), t[k][:], s[k][:], MULT)
            nc.sync.dma_start(out[k * P : (k + 1) * P, :], windows[k][:])
